import numpy as np
import ml_dtypes


def mxq(x, axis, fmt="e4m3"):
    dtype, down = {"e4m3": (ml_dtypes.float8_e4m3fn, 7), "e5m2": (ml_dtypes.float8_e5m2, 14)}[fmt]
    v = np.moveaxis(np.asarray(x, np.float32).astype(ml_dtypes.bfloat16).astype(np.float64), axis, -1)
    blocks = v.reshape(v.shape[:-1] + (-1, 32))
    amax = np.abs(blocks).max(-1, keepdims=True)
    byte = np.maximum(np.where(amax > 0, np.frexp(amax)[1] - 1 + 127, 0) - down, 1)
    scale = np.exp2(byte - 127.0)
    codes = (blocks / scale).astype(np.float32).astype(dtype).astype(np.float64)
    return np.moveaxis((codes * scale).reshape(v.shape), -1, axis)


WIDE = False


def mx_kscale(k):
    if not WIDE:
        return np.ones(k)
    levels = np.array([20, -20, 10, -10, 0])
    a = np.random.permutation(np.resize(levels, k // 512 * 4)).reshape(k // 512, 4)
    idx = np.arange(k)
    return np.exp2(a[idx // 512, idx % 128 // 32])


BF16 = ml_dtypes.bfloat16


def bf(x):
    return np.asarray(x, np.float32).astype(BF16)


def f64(x):
    return np.asarray(x).astype(np.float64)


B, S, D_IN, D_OUT = 4, 1024, 1024, 1024


def ternary(weight, alpha):
    w = f64(weight)
    delta = 0.7 * np.mean(np.abs(w))
    w_t = np.where(w > delta, 1.0, np.where(w < -delta, -1.0, 0.0))
    return w_t * f64(alpha)


def setup_inputs():
    u = mx_kscale(D_OUT)
    m = u.min()
    x = np.random.standard_normal((B, S, D_IN))
    weight = np.random.standard_normal((D_OUT, D_IN)) * 0.9 / np.sqrt(D_IN) * ((m / u) ** 2)[:, None]
    alpha = (1.0 + 0.1 * np.random.standard_normal(1)) * 1.3 / np.sqrt(D_IN) / m
    bias = np.random.standard_normal(D_OUT) * 0.1
    g = np.random.standard_normal((B, S, D_OUT)) * np.exp2(np.random.randint(-12, 1, (B, S, 1))) * 4.0 * u
    return {"x": bf(x), "weight": bf(weight), "alpha": bf(alpha), "bias": bf(bias), "grad_out": bf(g)}


def reference(x, weight, alpha, bias, grad_out):
    w_q = ternary(weight, alpha)
    return mxq(f64(grad_out), 2, "e5m2") @ mxq(w_q, 0, "e4m3")

@@ -1,0 +1,217 @@
+from contextlib import ExitStack
+
+from concourse import mybir
+from concourse.masks import make_identity
+
+F32 = mybir.dt.float32
+BF16 = mybir.dt.bfloat16
+U32 = mybir.dt.uint32
+U8 = mybir.dt.uint8
+I32 = mybir.dt.int32
+E4M3X4 = mybir.dt.float8_e4m3fn_x4
+E5M2X4 = mybir.dt.float8_e5m2_x4
+ALU = mybir.AluOpType
+
+P = 128
+TOKENS = 4096
+D_OUT = 1024
+D_IN = 1024
+PACK = 4
+K_PASS = P * PACK
+PASSES = D_OUT // K_PASS
+N_MX = 512
+HALVES = D_IN // N_MX
+TILES = TOKENS // P
+GROUP = 4
+GROUPS = TILES // GROUP
+LEAD = 7
+
+FLOPS = 2 * TOKENS * D_OUT * D_IN
+BYTES = TOKENS * D_OUT * 2 + D_OUT * D_IN * 2 + 2 + TOKENS * D_IN * 4
+
+
+def tile_ternarylinear_t_kernel(tc, x, weight, alpha, bias, grad_out, out):
+    nc = tc.nc
+    with ExitStack() as stack:
+        stack.enter_context(tc.manual_schedule())
+        const = stack.enter_context(tc.tile_pool(name="const", bufs=1))
+        keep = stack.enter_context(tc.tile_pool(name="keep", bufs=1))
+        work = stack.enter_context(tc.tile_pool(name="work", bufs=2))
+        g_pool = stack.enter_context(tc.tile_pool(name="g_pool", bufs=GROUPS + 1))
+        results = stack.enter_context(tc.tile_pool(name="results", bufs=6))
+        flipped = stack.enter_context(tc.psum_pool(name="flipped", bufs=4))
+        sums = stack.enter_context(tc.psum_pool(name="sums", bufs=4))
+
+        g_view = grad_out.flatten_outer_dims().rearrange("(p n) o -> p n o", n=TILES)
+        out_view = out.flatten_outer_dims().rearrange("(p n) d -> p n d", n=TILES)
+        w_view = weight.rearrange("(c u p e) d -> p c u (e d)", c=PASSES, u=2, p=P, e=2)
+
+        alpha_bf = const.tile([P, 1], BF16)
+        nc.scalar.dma_start(out=alpha_bf[:], in_=alpha.partition_broadcast(P))
+        w_raw = keep.tile([P, PASSES, PACK, D_IN], BF16)
+        for c in range(PASSES):
+            for u in range(2):
+                nc.sync.dma_start(
+                    out=w_raw[:, c, 2 * u : 2 * u + 2, :].rearrange("p e d -> p (e d)"),
+                    in_=w_view[:, c, u, :],
+                )
+        g_raw = []
+        for j in range(GROUPS):
+            g_tile = g_pool.tile([P, GROUP * D_OUT], BF16, align_bytes=64, name="g_tile")
+            for half in range(2):
+                first = GROUP * j + 2 * half
+                nc.sync.dma_start(
+                    out=g_tile[:, 2 * half * D_OUT : 2 * (half + 1) * D_OUT].rearrange(
+                        "p (n o) -> p n o", n=2
+                    ),
+                    in_=g_view[:, first : first + 2, :],
+                )
+            g_raw.append(g_tile)
+
+        identity = const.tile([P, P], F32)
+        make_identity(nc, identity[:])
+        ones = const.tile([P, P], BF16)
+        nc.vector.memset(ones[:], 1.0)
+
+        g_codes = keep.tile([P, GROUPS, GROUP * PASSES * P], U32, align_bytes=64)
+        g_scales = keep.tile([P, GROUPS, GROUP * PASSES * P], U8, align_bytes=64)
+        w_codes = keep.tile([P, PASSES, D_IN], U32, align_bytes=64)
+        w_scales = keep.tile([P, PASSES, D_IN], U8, align_bytes=64)
+        g_grouped = {}
+
+        def transpose_group(j):
+            words = g_raw[j][:].bitcast(F32)
+            grouped = g_pool.tile([P, GROUP * D_OUT], BF16, align_bytes=64, name="g_tile")
+            grouped_words = grouped[:].bitcast(F32).rearrange(
+                "p (n c m u) -> p n c m u", n=GROUP, c=PASSES, m=P, u=2
+            )
+            for n in range(GROUP):
+                bank = flipped.tile([P, PASSES * 2, P], F32, name="bank")
+                for cu in range(PASSES * 2):
+                    first = (n * PASSES * 2 + cu) * P
+                    nc.tensor.transpose(bank[:, cu, :], words[:, first : first + P], identity[:])
+                nc.scalar.copy(
+                    out=grouped_words[:, n],
+                    in_=bank[:].rearrange("p (c u) m -> p c m u", u=2),
+                )
+            g_grouped[j] = grouped
+
+        def quantise_group(j):
+            nc.vector.quantize_mx(
+                out=g_codes[:, j, :].bitcast(E5M2X4),
+                scales=g_scales[:, j, :],
+                in_=g_grouped[j][:],
+            )
+
+        def multiply_group(j):
+            for n in range(GROUP):
+                result = results.tile([P, D_IN], F32, name="result")
+                for h in range(HALVES):
+                    d_cols = slice(h * N_MX, (h + 1) * N_MX)
+                    acc = sums.tile([P, N_MX], F32, name="acc")
+                    for c in range(PASSES):
+                        m_cols = slice((n * PASSES + c) * P, (n * PASSES + c + 1) * P)
+                        nc.tensor.matmul_mx(
+                            out=acc[:],
+                            lhsT=g_codes[:, j, m_cols].bitcast(E5M2X4),
+                            lhsT_scale=g_scales[:, j, m_cols],
+                            rhs=w_codes[:, c, d_cols].bitcast(E4M3X4),
+                            rhs_scale=w_scales[:, c, d_cols],
+                            start=(c == 0),
+                            stop=(c == PASSES - 1),
+                        )
+                    if h == 0:
+                        nc.scalar.copy(out=result[:, d_cols], in_=acc[:])
+                    else:
+                        nc.vector.tensor_copy(out=result[:, d_cols], in_=acc[:])
+                nc.sync.dma_start(out=out_view[:, GROUP * j + n, :], in_=result[:])
+
+        w_abs = keep.tile([P, PASSES, PACK, D_IN], BF16)
+        w_grouped = keep.tile([P, PASSES, D_IN, PACK], BF16, align_bytes=64)
+        column_sums = sums.tile([P, N_MX], F32, name="acc")
+        for c in range(PASSES):
+            for u in range(2):
+                rows = slice(2 * u, 2 * u + 2)
+                nc.vector.tensor_single_scalar(
+                    out=w_abs[:, c, rows, :].rearrange("p e d -> p (e d)").bitcast(I32),
+                    in_=w_raw[:, c, rows, :].rearrange("p e d -> p (e d)").bitcast(I32),
+                    scalar=0x7FFF7FFF,
+                    op=ALU.bitwise_and,
+                )
+                for t in range(2 * u, 2 * u + 2):
+                    for h in range(HALVES):
+                        nc.tensor.matmul(
+                            out=column_sums[:],
+                            lhsT=ones[:],
+                            rhs=w_abs[:, c, t, h * N_MX : (h + 1) * N_MX],
+                            start=(c == 0 and t == 0 and h == 0),
+                            stop=(c == PASSES - 1 and t == PACK - 1 and h == HALVES - 1),
+                        )
+            nc.vector.tensor_copy(
+                out=w_grouped[:, c].rearrange("p (b i) t -> p b t i", i=4),
+                in_=w_raw[:, c].rearrange("p t (b i) -> p b t i", i=4),
+            )
+
+        transpose_group(0)
+
+        alpha_f32 = const.tile([P, 1], F32)
+        nc.vector.tensor_copy(out=alpha_f32[:], in_=alpha_bf[:])
+        total = const.tile([P, 1], F32)
+        nc.vector.tensor_reduce(
+            out=total[:], in_=column_sums[:], axis=mybir.AxisListType.X, op=ALU.add
+        )
+        delta = const.tile([P, 1], F32)
+        nc.vector.tensor_scalar_mul(out=delta[:], in0=total[:], scalar1=0.7 / (D_OUT * D_IN))
+        minus_delta = const.tile([P, 1], F32)
+        nc.vector.tensor_scalar_mul(
+            out=minus_delta[:], in0=total[:], scalar1=-0.7 / (D_OUT * D_IN)
+        )
+
+        for j in range(1, LEAD):
+            transpose_group(j)
+
+        quarters = [(c, h) for h in range(HALVES) for c in range(PASSES)]
+        w_q = {}
+
+        def quantise_quarter(c, h):
+            d_cols = slice(h * N_MX, (h + 1) * N_MX)
+            nc.vector.quantize_mx(
+                out=w_codes[:, c, d_cols].bitcast(E4M3X4),
+                scales=w_scales[:, c, d_cols],
+                in_=w_q[(c, h)][:],
+            )
+
+        for index, (c, h) in enumerate(quarters):
+            values = w_grouped[:, c, h * N_MX : (h + 1) * N_MX, :].rearrange("p d t -> p (d t)")
+            above = work.tile([P, N_MX * PACK], BF16, name="above")
+            nc.vector.tensor_scalar(
+                out=above[:],
+                in0=values,
+                scalar1=delta[:, 0:1],
+                scalar2=alpha_f32[:, 0:1],
+                op0=ALU.is_gt,
+                op1=ALU.mult,
+            )
+            below = work.tile([P, N_MX * PACK], BF16, name="below")
+            nc.vector.tensor_scalar(
+                out=below[:],
+                in0=values,
+                scalar1=minus_delta[:, 0:1],
+                scalar2=alpha_f32[:, 0:1],
+                op0=ALU.is_lt,
+                op1=ALU.mult,
+            )
+            ternary = work.tile([P, N_MX * PACK], BF16, align_bytes=64, name="ternary")
+            nc.vector.tensor_tensor(out=ternary[:], in0=above[:], in1=below[:], op=ALU.subtract)
+            w_q[(c, h)] = ternary
+            if index > 0:
+                quantise_quarter(*quarters[index - 1])
+        quantise_quarter(*quarters[-1])
+
+        quantise_group(0)
+        for j in range(GROUPS):
+            if j + LEAD < GROUPS:
+                transpose_group(j + LEAD)
+            if j + 1 < GROUPS:
+                quantise_group(j + 1)
+            multiply_group(j)

@@ -24,7 +24,7 @@ HALVES = D_IN // N_MX
 TILES = TOKENS // P
 GROUP = 4
 GROUPS = TILES // GROUP
-LEAD = 7
+LEAD = 5
 
 FLOPS = 2 * TOKENS * D_OUT * D_IN
 BYTES = TOKENS * D_OUT * 2 + D_OUT * D_IN * 2 + 2 + TOKENS * D_IN * 4
@@ -147,9 +147,13 @@ def tile_ternarylinear_t_kernel(tc, x, weight, alpha, bias, grad_out, out):
                             start=(c == 0 and t == 0 and h == 0),
                             stop=(c == PASSES - 1 and t == PACK - 1 and h == HALVES - 1),
                         )
+            nc.scalar.copy(
+                out=w_grouped[:, c, 0:N_MX, :].rearrange("p (b i) t -> p b t i", i=4),
+                in_=w_raw[:, c, :, 0:N_MX].rearrange("p t (b i) -> p b t i", i=4),
+            )
             nc.vector.tensor_copy(
-                out=w_grouped[:, c].rearrange("p (b i) t -> p b t i", i=4),
-                in_=w_raw[:, c].rearrange("p t (b i) -> p b t i", i=4),
+                out=w_grouped[:, c, N_MX:D_IN, :].rearrange("p (b i) t -> p b t i", i=4),
+                in_=w_raw[:, c, :, N_MX:D_IN].rearrange("p t (b i) -> p b t i", i=4),
             )
 
         transpose_group(0)
@@ -210,8 +214,8 @@ def tile_ternarylinear_t_kernel(tc, x, weight, alpha, bias, grad_out, out):
 
         quantise_group(0)
         for j in range(GROUPS):
-            if j + LEAD < GROUPS:
-                transpose_group(j + LEAD)
             if j + 1 < GROUPS:
                 quantise_group(j + 1)
             multiply_group(j)
+            if j + LEAD < GROUPS:
+                transpose_group(j + LEAD)

@@ -24,7 +24,8 @@ HALVES = D_IN // N_MX
 TILES = TOKENS // P
 GROUP = 4
 GROUPS = TILES // GROUP
-LEAD = 5
+LEAD = 4
+PIECE = 256
 
 FLOPS = 2 * TOKENS * D_OUT * D_IN
 BYTES = TOKENS * D_OUT * 2 + D_OUT * D_IN * 2 + 2 + TOKENS * D_IN * 4
@@ -38,7 +39,7 @@ def tile_ternarylinear_t_kernel(tc, x, weight, alpha, bias, grad_out, out):
         keep = stack.enter_context(tc.tile_pool(name="keep", bufs=1))
         work = stack.enter_context(tc.tile_pool(name="work", bufs=2))
         g_pool = stack.enter_context(tc.tile_pool(name="g_pool", bufs=GROUPS + 1))
-        results = stack.enter_context(tc.tile_pool(name="results", bufs=6))
+        results = stack.enter_context(tc.tile_pool(name="results", bufs=8))
         flipped = stack.enter_context(tc.psum_pool(name="flipped", bufs=4))
         sums = stack.enter_context(tc.psum_pool(name="sums", bufs=4))
 
@@ -103,28 +104,27 @@ def tile_ternarylinear_t_kernel(tc, x, weight, alpha, bias, grad_out, out):
                 in_=g_grouped[j][:],
             )
 
-        def multiply_group(j):
+        def multiply_group(j, h):
+            d_cols = slice(h * N_MX, (h + 1) * N_MX)
             for n in range(GROUP):
-                result = results.tile([P, D_IN], F32, name="result")
-                for h in range(HALVES):
-                    d_cols = slice(h * N_MX, (h + 1) * N_MX)
-                    acc = sums.tile([P, N_MX], F32, name="acc")
-                    for c in range(PASSES):
-                        m_cols = slice((n * PASSES + c) * P, (n * PASSES + c + 1) * P)
-                        nc.tensor.matmul_mx(
-                            out=acc[:],
-                            lhsT=g_codes[:, j, m_cols].bitcast(E5M2X4),
-                            lhsT_scale=g_scales[:, j, m_cols],
-                            rhs=w_codes[:, c, d_cols].bitcast(E4M3X4),
-                            rhs_scale=w_scales[:, c, d_cols],
-                            start=(c == 0),
-                            stop=(c == PASSES - 1),
-                        )
-                    if h == 0:
-                        nc.scalar.copy(out=result[:, d_cols], in_=acc[:])
-                    else:
-                        nc.vector.tensor_copy(out=result[:, d_cols], in_=acc[:])
-                nc.sync.dma_start(out=out_view[:, GROUP * j + n, :], in_=result[:])
+                acc = sums.tile([P, N_MX], F32, name="acc")
+                for c in range(PASSES):
+                    m_cols = slice((n * PASSES + c) * P, (n * PASSES + c + 1) * P)
+                    nc.tensor.matmul_mx(
+                        out=acc[:],
+                        lhsT=g_codes[:, j, m_cols].bitcast(E5M2X4),
+                        lhsT_scale=g_scales[:, j, m_cols],
+                        rhs=w_codes[:, c, d_cols].bitcast(E4M3X4),
+                        rhs_scale=w_scales[:, c, d_cols],
+                        start=(c == 0),
+                        stop=(c == PASSES - 1),
+                    )
+                result = results.tile([P, N_MX], F32, name="result")
+                if n % 2 == 0:
+                    nc.scalar.copy(out=result[:], in_=acc[:])
+                else:
+                    nc.vector.tensor_copy(out=result[:], in_=acc[:])
+                nc.sync.dma_start(out=out_view[:, GROUP * j + n, d_cols], in_=result[:])
 
         w_abs = keep.tile([P, PASSES, PACK, D_IN], BF16)
         w_grouped = keep.tile([P, PASSES, D_IN, PACK], BF16, align_bytes=64)
@@ -174,20 +174,9 @@ def tile_ternarylinear_t_kernel(tc, x, weight, alpha, bias, grad_out, out):
         for j in range(1, LEAD):
             transpose_group(j)
 
-        quarters = [(c, h) for h in range(HALVES) for c in range(PASSES)]
-        w_q = {}
-
-        def quantise_quarter(c, h):
-            d_cols = slice(h * N_MX, (h + 1) * N_MX)
-            nc.vector.quantize_mx(
-                out=w_codes[:, c, d_cols].bitcast(E4M3X4),
-                scales=w_scales[:, c, d_cols],
-                in_=w_q[(c, h)][:],
-            )
-
-        for index, (c, h) in enumerate(quarters):
-            values = w_grouped[:, c, h * N_MX : (h + 1) * N_MX, :].rearrange("p d t -> p (d t)")
-            above = work.tile([P, N_MX * PACK], BF16, name="above")
+        def ternarise(c, first, width):
+            values = w_grouped[:, c, first : first + width, :].rearrange("p d t -> p (d t)")
+            above = work.tile([P, width * PACK], BF16, name="above")
             nc.vector.tensor_scalar(
                 out=above[:],
                 in0=values,
@@ -196,7 +185,7 @@ def tile_ternarylinear_t_kernel(tc, x, weight, alpha, bias, grad_out, out):
                 op0=ALU.is_gt,
                 op1=ALU.mult,
             )
-            below = work.tile([P, N_MX * PACK], BF16, name="below")
+            below = work.tile([P, width * PACK], BF16, name="below")
             nc.vector.tensor_scalar(
                 out=below[:],
                 in0=values,
@@ -205,17 +194,34 @@ def tile_ternarylinear_t_kernel(tc, x, weight, alpha, bias, grad_out, out):
                 op0=ALU.is_lt,
                 op1=ALU.mult,
             )
-            ternary = work.tile([P, N_MX * PACK], BF16, align_bytes=64, name="ternary")
+            ternary = work.tile([P, width * PACK], BF16, align_bytes=64, name="ternary")
             nc.vector.tensor_tensor(out=ternary[:], in0=above[:], in1=below[:], op=ALU.subtract)
-            w_q[(c, h)] = ternary
-            if index > 0:
-                quantise_quarter(*quarters[index - 1])
-        quantise_quarter(*quarters[-1])
+            return ternary
 
+        def quantise_weight(c, first, width, ternary):
+            nc.vector.quantize_mx(
+                out=w_codes[:, c, first : first + width].bitcast(E4M3X4),
+                scales=w_scales[:, c, first : first + width],
+                in_=ternary[:],
+            )
+
+        left = [ternarise(c, 0, N_MX) for c in range(PASSES)]
+        for c in range(PASSES):
+            quantise_weight(c, 0, N_MX, left[c])
         quantise_group(0)
+
+        pieces = [
+            (c, first) for c in range(PASSES) for first in range(N_MX, D_IN, PIECE)
+        ]
         for j in range(GROUPS):
             if j + 1 < GROUPS:
                 quantise_group(j + 1)
-            multiply_group(j)
+            if j < len(pieces):
+                right = ternarise(pieces[j][0], pieces[j][1], PIECE)
+            multiply_group(j, 0)
+            if j < len(pieces):
+                quantise_weight(pieces[j][0], pieces[j][1], PIECE, right)
             if j + LEAD < GROUPS:
                 transpose_group(j + LEAD)
+        for j in range(GROUPS):
+            multiply_group(j, 1)

@@ -24,8 +24,13 @@ HALVES = D_IN // N_MX
 TILES = TOKENS // P
 GROUP = 4
 GROUPS = TILES // GROUP
-LEAD = 4
+AHEAD = 6
+HALF = 2
+UNITS = TILES // HALF
+LEAD = 8
 PIECE = 256
+EARLY = 6
+WARM = 4
 
 FLOPS = 2 * TOKENS * D_OUT * D_IN
 BYTES = TOKENS * D_OUT * 2 + D_OUT * D_IN * 2 + 2 + TOKENS * D_IN * 4
@@ -38,10 +43,10 @@ def tile_ternarylinear_t_kernel(tc, x, weight, alpha, bias, grad_out, out):
         const = stack.enter_context(tc.tile_pool(name="const", bufs=1))
         keep = stack.enter_context(tc.tile_pool(name="keep", bufs=1))
         work = stack.enter_context(tc.tile_pool(name="work", bufs=2))
-        g_pool = stack.enter_context(tc.tile_pool(name="g_pool", bufs=GROUPS + 1))
-        results = stack.enter_context(tc.tile_pool(name="results", bufs=8))
-        flipped = stack.enter_context(tc.psum_pool(name="flipped", bufs=4))
-        sums = stack.enter_context(tc.psum_pool(name="sums", bufs=4))
+        g_pool = stack.enter_context(tc.tile_pool(name="g_pool", bufs=UNITS + 2))
+        results = stack.enter_context(tc.tile_pool(name="results", bufs=16))
+        flipped = stack.enter_context(tc.psum_pool(name="flipped", bufs=3))
+        sums = stack.enter_context(tc.psum_pool(name="sums", bufs=5))
 
         g_view = grad_out.flatten_outer_dims().rearrange("(p n) o -> p n o", n=TILES)
         out_view = out.flatten_outer_dims().rearrange("(p n) d -> p n d", n=TILES)
@@ -57,36 +62,38 @@ def tile_ternarylinear_t_kernel(tc, x, weight, alpha, bias, grad_out, out):
                     in_=w_view[:, c, u, :],
                 )
         g_raw = []
-        for j in range(GROUPS):
-            g_tile = g_pool.tile([P, GROUP * D_OUT], BF16, align_bytes=64, name="g_tile")
-            for half in range(2):
-                first = GROUP * j + 2 * half
-                nc.sync.dma_start(
-                    out=g_tile[:, 2 * half * D_OUT : 2 * (half + 1) * D_OUT].rearrange(
-                        "p (n o) -> p n o", n=2
-                    ),
-                    in_=g_view[:, first : first + 2, :],
-                )
+        for unit in range(UNITS):
+            g_tile = g_pool.tile([P, HALF * D_OUT], BF16, align_bytes=64, name="g_tile")
+            nc.sync.dma_start(
+                out=g_tile[:].rearrange("p (n o) -> p n o", n=HALF),
+                in_=g_view[:, HALF * unit : HALF * (unit + 1), :],
+            )
             g_raw.append(g_tile)
 
+        ones = const.tile([P, N_MX], BF16)
+        nc.vector.memset(ones[:], 1.0)
+        table = const.tile([P, 1], BF16)
+        nc.scalar.copy(out=table[:], in_=ones[:, 0:1])
         identity = const.tile([P, P], F32)
         make_identity(nc, identity[:])
-        ones = const.tile([P, P], BF16)
-        nc.vector.memset(ones[:], 1.0)
 
-        g_codes = keep.tile([P, GROUPS, GROUP * PASSES * P], U32, align_bytes=64)
-        g_scales = keep.tile([P, GROUPS, GROUP * PASSES * P], U8, align_bytes=64)
+        warm = sums.tile([P, N_MX], F32, name="acc")
+        for i in range(WARM):
+            nc.tensor.matmul(out=warm[:], lhsT=ones[:, 0:P], rhs=ones[:], start=True, stop=True)
+
+        g_codes = keep.tile([P, UNITS, HALF * PASSES * P], U32, align_bytes=64)
+        g_scales = keep.tile([P, UNITS, HALF * PASSES * P], U8, align_bytes=64)
         w_codes = keep.tile([P, PASSES, D_IN], U32, align_bytes=64)
         w_scales = keep.tile([P, PASSES, D_IN], U8, align_bytes=64)
         g_grouped = {}
 
-        def transpose_group(j):
-            words = g_raw[j][:].bitcast(F32)
-            grouped = g_pool.tile([P, GROUP * D_OUT], BF16, align_bytes=64, name="g_tile")
+        def transpose_unit(unit):
+            words = g_raw[unit][:].bitcast(F32)
+            grouped = g_pool.tile([P, HALF * D_OUT], BF16, align_bytes=64, name="g_tile")
             grouped_words = grouped[:].bitcast(F32).rearrange(
-                "p (n c m u) -> p n c m u", n=GROUP, c=PASSES, m=P, u=2
+                "p (n c m u) -> p n c m u", n=HALF, c=PASSES, m=P, u=2
             )
-            for n in range(GROUP):
+            for n in range(HALF):
                 bank = flipped.tile([P, PASSES * 2, P], F32, name="bank")
                 for cu in range(PASSES * 2):
                     first = (n * PASSES * 2 + cu) * P
@@ -95,68 +102,89 @@ def tile_ternarylinear_t_kernel(tc, x, weight, alpha, bias, grad_out, out):
                     out=grouped_words[:, n],
                     in_=bank[:].rearrange("p (c u) m -> p c m u", u=2),
                 )
-            g_grouped[j] = grouped
+            g_grouped[unit] = grouped
 
-        def quantise_group(j):
+        def quantise_unit(unit):
             nc.vector.quantize_mx(
-                out=g_codes[:, j, :].bitcast(E5M2X4),
-                scales=g_scales[:, j, :],
-                in_=g_grouped[j][:],
+                out=g_codes[:, unit, :].bitcast(E5M2X4),
+                scales=g_scales[:, unit, :],
+                in_=g_grouped[unit][:],
             )
 
-        def multiply_group(j, h):
+        def multiply(acc, tile, c, h):
             d_cols = slice(h * N_MX, (h + 1) * N_MX)
-            for n in range(GROUP):
-                acc = sums.tile([P, N_MX], F32, name="acc")
-                for c in range(PASSES):
-                    m_cols = slice((n * PASSES + c) * P, (n * PASSES + c + 1) * P)
-                    nc.tensor.matmul_mx(
-                        out=acc[:],
-                        lhsT=g_codes[:, j, m_cols].bitcast(E5M2X4),
-                        lhsT_scale=g_scales[:, j, m_cols],
-                        rhs=w_codes[:, c, d_cols].bitcast(E4M3X4),
-                        rhs_scale=w_scales[:, c, d_cols],
-                        start=(c == 0),
-                        stop=(c == PASSES - 1),
-                    )
-                result = results.tile([P, N_MX], F32, name="result")
-                if n % 2 == 0:
-                    nc.scalar.copy(out=result[:], in_=acc[:])
-                else:
-                    nc.vector.tensor_copy(out=result[:], in_=acc[:])
-                nc.sync.dma_start(out=out_view[:, GROUP * j + n, d_cols], in_=result[:])
+            first = (tile % HALF * PASSES + c) * P
+            m_cols = slice(first, first + P)
+            nc.tensor.matmul_mx(
+                out=acc[:],
+                lhsT=g_codes[:, tile // HALF, m_cols].bitcast(E5M2X4),
+                lhsT_scale=g_scales[:, tile // HALF, m_cols],
+                rhs=w_codes[:, c, d_cols].bitcast(E4M3X4),
+                rhs_scale=w_scales[:, c, d_cols],
+                start=(c == 0),
+                stop=(c == PASSES - 1),
+            )
+
+        def store(acc, tile, h, on_scalar):
+            result = results.tile([P, N_MX], F32, name="result")
+            if on_scalar:
+                nc.scalar.copy(out=result[:], in_=acc[:])
+            else:
+                nc.vector.tensor_copy(out=result[:], in_=acc[:])
+            nc.sync.dma_start(
+                out=out_view[:, tile, h * N_MX : (h + 1) * N_MX], in_=result[:]
+            )
 
         w_abs = keep.tile([P, PASSES, PACK, D_IN], BF16)
         w_grouped = keep.tile([P, PASSES, D_IN, PACK], BF16, align_bytes=64)
         column_sums = sums.tile([P, N_MX], F32, name="acc")
-        for c in range(PASSES):
-            for u in range(2):
-                rows = slice(2 * u, 2 * u + 2)
-                nc.vector.tensor_single_scalar(
-                    out=w_abs[:, c, rows, :].rearrange("p e d -> p (e d)").bitcast(I32),
-                    in_=w_raw[:, c, rows, :].rearrange("p e d -> p (e d)").bitcast(I32),
-                    scalar=0x7FFF7FFF,
-                    op=ALU.bitwise_and,
-                )
-                for t in range(2 * u, 2 * u + 2):
-                    for h in range(HALVES):
-                        nc.tensor.matmul(
-                            out=column_sums[:],
-                            lhsT=ones[:],
-                            rhs=w_abs[:, c, t, h * N_MX : (h + 1) * N_MX],
-                            start=(c == 0 and t == 0 and h == 0),
-                            stop=(c == PASSES - 1 and t == PACK - 1 and h == HALVES - 1),
-                        )
-            nc.scalar.copy(
-                out=w_grouped[:, c, 0:N_MX, :].rearrange("p (b i) t -> p b t i", i=4),
-                in_=w_raw[:, c, :, 0:N_MX].rearrange("p t (b i) -> p b t i", i=4),
+
+        def add_chunk(c, u):
+            rows = slice(2 * u, 2 * u + 2)
+            nc.vector.tensor_single_scalar(
+                out=w_abs[:, c, rows, :].rearrange("p e d -> p (e d)").bitcast(I32),
+                in_=w_raw[:, c, rows, :].rearrange("p e d -> p (e d)").bitcast(I32),
+                scalar=0x7FFF7FFF,
+                op=ALU.bitwise_and,
             )
-            nc.vector.tensor_copy(
-                out=w_grouped[:, c, N_MX:D_IN, :].rearrange("p (b i) t -> p b t i", i=4),
-                in_=w_raw[:, c, :, N_MX:D_IN].rearrange("p t (b i) -> p b t i", i=4),
+            for t in range(2 * u, 2 * u + 2):
+                for h in range(HALVES):
+                    nc.tensor.matmul(
+                        out=column_sums[:],
+                        lhsT=ones[:, 0:P],
+                        rhs=w_abs[:, c, t, h * N_MX : (h + 1) * N_MX],
+                        start=(c == 0 and t == 0 and h == 0),
+                        stop=(c == PASSES - 1 and t == PACK - 1 and h == HALVES - 1),
+                    )
+
+        def regroup(copy, c, first, width):
+            copy(
+                out=w_grouped[:, c, first : first + width, :].rearrange(
+                    "p (b i) t -> p b t i", i=4
+                ),
+                in_=w_raw[:, c, :, first : first + width].rearrange("p t (b i) -> p b t i", i=4),
             )
 
-        transpose_group(0)
+        def magnitudes(c, first, width):
+            magnitude = work.tile([P, width * PACK], BF16, name="magnitude")
+            nc.vector.tensor_single_scalar(
+                out=magnitude[:].bitcast(I32),
+                in_=w_grouped[:, c, first : first + width, :]
+                .rearrange("p d t -> p (d t)")
+                .bitcast(I32),
+                scalar=0x7FFF7FFF,
+                op=ALU.bitwise_and,
+            )
+            return magnitude
+
+        add_chunk(0, 0)
+        add_chunk(0, 1)
+        regroup(nc.scalar.copy, 0, 0, N_MX)
+        add_chunk(1, 0)
+        add_chunk(1, 1)
+        regroup(nc.scalar.copy, 1, 0, N_MX)
+        magnitude = magnitudes(0, 0, N_MX)
+        regroup(nc.vector.tensor_copy, 0, N_MX, PIECE)
 
         alpha_f32 = const.tile([P, 1], F32)
         nc.vector.tensor_copy(out=alpha_f32[:], in_=alpha_bf[:])
@@ -166,36 +194,31 @@ def tile_ternarylinear_t_kernel(tc, x, weight, alpha, bias, grad_out, out):
         )
         delta = const.tile([P, 1], F32)
         nc.vector.tensor_scalar_mul(out=delta[:], in0=total[:], scalar1=0.7 / (D_OUT * D_IN))
-        minus_delta = const.tile([P, 1], F32)
-        nc.vector.tensor_scalar_mul(
-            out=minus_delta[:], in0=total[:], scalar1=-0.7 / (D_OUT * D_IN)
-        )
 
-        for j in range(1, LEAD):
-            transpose_group(j)
-
-        def ternarise(c, first, width):
-            values = w_grouped[:, c, first : first + width, :].rearrange("p d t -> p (d t)")
-            above = work.tile([P, width * PACK], BF16, name="above")
+        def masks(width, magnitude):
+            mask = work.tile([P, width * PACK], BF16, name="mask")
             nc.vector.tensor_scalar(
-                out=above[:],
-                in0=values,
+                out=mask[:],
+                in0=magnitude[:],
                 scalar1=delta[:, 0:1],
                 scalar2=alpha_f32[:, 0:1],
                 op0=ALU.is_gt,
                 op1=ALU.mult,
             )
-            below = work.tile([P, width * PACK], BF16, name="below")
-            nc.vector.tensor_scalar(
-                out=below[:],
-                in0=values,
-                scalar1=minus_delta[:, 0:1],
-                scalar2=alpha_f32[:, 0:1],
-                op0=ALU.is_lt,
-                op1=ALU.mult,
-            )
+            return mask
+
+        def ternarise(c, first, width, mask):
             ternary = work.tile([P, width * PACK], BF16, align_bytes=64, name="ternary")
-            nc.vector.tensor_tensor(out=ternary[:], in0=above[:], in1=below[:], op=ALU.subtract)
+            nc.vector.scalar_tensor_tensor(
+                out=ternary[:].bitcast(I32),
+                in0=w_grouped[:, c, first : first + width, :]
+                .rearrange("p d t -> p (d t)")
+                .bitcast(I32),
+                scalar=-0x7FFF8000,
+                in1=mask[:].bitcast(I32),
+                op0=ALU.bitwise_and,
+                op1=ALU.bitwise_xor,
+            )
             return ternary
 
         def quantise_weight(c, first, width, ternary):
@@ -205,23 +228,71 @@ def tile_ternarylinear_t_kernel(tc, x, weight, alpha, bias, grad_out, out):
                 in_=ternary[:],
             )
 
-        left = [ternarise(c, 0, N_MX) for c in range(PASSES)]
-        for c in range(PASSES):
-            quantise_weight(c, 0, N_MX, left[c])
-        quantise_group(0)
+        for unit in range(AHEAD):
+            transpose_unit(unit)
 
-        pieces = [
-            (c, first) for c in range(PASSES) for first in range(N_MX, D_IN, PIECE)
-        ]
+        mask = masks(N_MX, magnitude)
+        magnitude = magnitudes(1, 0, N_MX)
+        left = ternarise(0, 0, N_MX, mask)
+        quantise_unit(0)
+        quantise_weight(0, 0, N_MX, left)
+        mask = masks(N_MX, magnitude)
+        quantise_unit(1)
+        left = ternarise(1, 0, N_MX, mask)
+
+        pieces = [(c, first) for c in range(PASSES) for first in range(N_MX, D_IN, PIECE)]
+        ready = {}
+
+        def weight_step(number):
+            if number < len(pieces) - 1:
+                c, first = pieces[number + 1]
+                regroup(nc.vector.tensor_copy, c, first, PIECE)
+                return
+            i, odd = divmod(number - (len(pieces) - 1), 2)
+            if odd:
+                if i < len(pieces):
+                    c, first = pieces[i]
+                    ready["ternary"] = ternarise(c, first, PIECE, ready["mask"])
+                return
+            if 0 < i <= len(pieces):
+                c, first = pieces[i - 1]
+                quantise_weight(c, first, PIECE, ready["ternary"])
+            if i < len(pieces):
+                c, first = pieces[i]
+                ready["mask"] = masks(PIECE, magnitudes(c, first, PIECE))
+
+        accs = []
+        for tile in range(GROUP):
+            acc = sums.tile([P, N_MX], F32, name="acc")
+            multiply(acc, tile, 0, 0)
+            accs.append(acc)
+        for unit in range(AHEAD, LEAD):
+            transpose_unit(unit)
+        quantise_weight(1, 0, N_MX, left)
+
+        blocks = [(0, j) for j in range(EARLY)]
         for j in range(GROUPS):
-            if j + 1 < GROUPS:
-                quantise_group(j + 1)
-            if j < len(pieces):
-                right = ternarise(pieces[j][0], pieces[j][1], PIECE)
-            multiply_group(j, 0)
-            if j < len(pieces):
-                quantise_weight(pieces[j][0], pieces[j][1], PIECE, right)
-            if j + LEAD < GROUPS:
-                transpose_group(j + LEAD)
-        for j in range(GROUPS):
-            multiply_group(j, 1)
+            blocks.append((1, j))
+            if EARLY + j < GROUPS:
+                blocks.append((0, EARLY + j))
+        next_unit = LEAD
+        number = 0
+        for b, (h, j) in enumerate(blocks):
+            for i in range(GROUP):
+                tile = GROUP * j + i
+                if b == 0:
+                    acc = accs[i]
+                    multiply(acc, tile, 1, 0)
+                else:
+                    acc = sums.tile([P, N_MX], F32, name="acc")
+                    for c in range(PASSES):
+                        multiply(acc, tile, c, h)
+                if i % 2 == 0 and b + 1 < len(blocks) and blocks[b + 1][0] == 0:
+                    quantise_unit(2 * blocks[b + 1][1] + i // 2)
+                if i % 2 == 1 and b < EARLY:
+                    weight_step(number)
+                    number += 1
+                store(acc, tile, h, i % 2 == 0 or (b < EARLY and i == 1))
+            if next_unit < UNITS:
+                transpose_unit(next_unit)
+                next_unit += 1

@@ -29,7 +29,9 @@ HALF = 2
 UNITS = TILES // HALF
 LEAD = 8
 PIECE = 256
+BETWEEN = ((6,), (7,))
 EARLY = 6
+N_SUM = 256
 WARM = 4
 
 FLOPS = 2 * TOKENS * D_OUT * D_IN
@@ -42,9 +44,10 @@ def tile_ternarylinear_t_kernel(tc, x, weight, alpha, bias, grad_out, out):
         stack.enter_context(tc.manual_schedule())
         const = stack.enter_context(tc.tile_pool(name="const", bufs=1))
         keep = stack.enter_context(tc.tile_pool(name="keep", bufs=1))
-        work = stack.enter_context(tc.tile_pool(name="work", bufs=2))
-        g_pool = stack.enter_context(tc.tile_pool(name="g_pool", bufs=UNITS + 2))
-        results = stack.enter_context(tc.tile_pool(name="results", bufs=16))
+        work = stack.enter_context(tc.tile_pool(name="work", bufs=3))
+        g_pool = stack.enter_context(tc.tile_pool(name="g_pool", bufs=GROUPS + 1))
+        results = stack.enter_context(tc.tile_pool(name="results", bufs=4))
+        half_rows = stack.enter_context(tc.tile_pool(name="half_rows", bufs=20))
         flipped = stack.enter_context(tc.psum_pool(name="flipped", bufs=3))
         sums = stack.enter_context(tc.psum_pool(name="sums", bufs=5))
 
@@ -54,20 +57,30 @@ def tile_ternarylinear_t_kernel(tc, x, weight, alpha, bias, grad_out, out):
 
         alpha_bf = const.tile([P, 1], BF16)
         nc.scalar.dma_start(out=alpha_bf[:], in_=alpha.partition_broadcast(P))
-        w_raw = keep.tile([P, PASSES, PACK, D_IN], BF16)
+        w_raw = []
         for c in range(PASSES):
+            w_tile = results.tile([P, PACK, D_IN], BF16, name="result")
             for u in range(2):
-                nc.sync.dma_start(
-                    out=w_raw[:, c, 2 * u : 2 * u + 2, :].rearrange("p e d -> p (e d)"),
-                    in_=w_view[:, c, u, :],
-                )
+                halves = 2 if c == PASSES - 1 and u == 1 else 1
+                width = 2 // halves
+                for e in range(0, 2, width):
+                    t = 2 * u + e
+                    nc.sync.dma_start(
+                        out=w_tile[:, t : t + width, :].rearrange("p e d -> p (e d)"),
+                        in_=w_view[:, c, u, e * D_IN : (e + width) * D_IN],
+                    )
+            w_raw.append(w_tile)
         g_raw = []
-        for unit in range(UNITS):
-            g_tile = g_pool.tile([P, HALF * D_OUT], BF16, align_bytes=64, name="g_tile")
-            nc.sync.dma_start(
-                out=g_tile[:].rearrange("p (n o) -> p n o", n=HALF),
-                in_=g_view[:, HALF * unit : HALF * (unit + 1), :],
-            )
+        for j in range(GROUPS):
+            g_tile = g_pool.tile([P, GROUP * D_OUT], BF16, align_bytes=64, name="g_tile")
+            tiles_a_load = HALF if j < GROUPS // 2 else GROUP
+            for n in range(0, GROUP, tiles_a_load):
+                nc.sync.dma_start(
+                    out=g_tile[:, n * D_OUT : (n + tiles_a_load) * D_OUT].rearrange(
+                        "p (n o) -> p n o", n=tiles_a_load
+                    ),
+                    in_=g_view[:, GROUP * j + n : GROUP * j + n + tiles_a_load, :],
+                )
             g_raw.append(g_tile)
 
         ones = const.tile([P, N_MX], BF16)
@@ -88,27 +101,32 @@ def tile_ternarylinear_t_kernel(tc, x, weight, alpha, bias, grad_out, out):
         g_grouped = {}
 
         def transpose_unit(unit):
-            words = g_raw[unit][:].bitcast(F32)
-            grouped = g_pool.tile([P, HALF * D_OUT], BF16, align_bytes=64, name="g_tile")
-            grouped_words = grouped[:].bitcast(F32).rearrange(
+            j, half = divmod(unit, GROUP // HALF)
+            words = g_raw[j][:].bitcast(F32)
+            if half == 0:
+                g_grouped[j] = g_pool.tile(
+                    [P, GROUP * D_OUT], BF16, align_bytes=64, name="g_tile"
+                )
+            grouped_words = g_grouped[j][:, half * HALF * D_OUT : (half + 1) * HALF * D_OUT].bitcast(F32).rearrange(
                 "p (n c m u) -> p n c m u", n=HALF, c=PASSES, m=P, u=2
             )
             for n in range(HALF):
                 bank = flipped.tile([P, PASSES * 2, P], F32, name="bank")
                 for cu in range(PASSES * 2):
-                    first = (n * PASSES * 2 + cu) * P
+                    first = ((half * HALF + n) * PASSES * 2 + cu) * P
                     nc.tensor.transpose(bank[:, cu, :], words[:, first : first + P], identity[:])
                 nc.scalar.copy(
                     out=grouped_words[:, n],
                     in_=bank[:].rearrange("p (c u) m -> p c m u", u=2),
                 )
-            g_grouped[unit] = grouped
 
         def quantise_unit(unit):
             nc.vector.quantize_mx(
                 out=g_codes[:, unit, :].bitcast(E5M2X4),
                 scales=g_scales[:, unit, :],
-                in_=g_grouped[unit][:],
+                in_=g_grouped[unit // 2][
+                    :, unit % 2 * HALF * D_OUT : (unit % 2 + 1) * HALF * D_OUT
+                ],
             )
 
         def multiply(acc, tile, c, h):
@@ -126,35 +144,34 @@ def tile_ternarylinear_t_kernel(tc, x, weight, alpha, bias, grad_out, out):
             )
 
         def store(acc, tile, h, on_scalar):
-            result = results.tile([P, N_MX], F32, name="result")
+            d_cols = slice(h * N_MX, (h + 1) * N_MX)
+            result = half_rows.tile([P, N_MX], F32, name="half_row")
             if on_scalar:
                 nc.scalar.copy(out=result[:], in_=acc[:])
             else:
                 nc.vector.tensor_copy(out=result[:], in_=acc[:])
-            nc.sync.dma_start(
-                out=out_view[:, tile, h * N_MX : (h + 1) * N_MX], in_=result[:]
-            )
+            nc.sync.dma_start(out=out_view[:, tile, d_cols], in_=result[:])
 
-        w_abs = keep.tile([P, PASSES, PACK, D_IN], BF16)
+        w_abs = [results.tile([P, PACK, D_IN], BF16, name="result") for c in range(PASSES)]
         w_grouped = keep.tile([P, PASSES, D_IN, PACK], BF16, align_bytes=64)
-        column_sums = sums.tile([P, N_MX], F32, name="acc")
+        column_sums = sums.tile([P, N_SUM], F32, name="acc")
 
-        def add_chunk(c, u):
-            rows = slice(2 * u, 2 * u + 2)
+        def add_chunk(c, first, width):
+            values = slice(first, first + width)
             nc.vector.tensor_single_scalar(
-                out=w_abs[:, c, rows, :].rearrange("p e d -> p (e d)").bitcast(I32),
-                in_=w_raw[:, c, rows, :].rearrange("p e d -> p (e d)").bitcast(I32),
+                out=w_abs[c][:, values, :].rearrange("p t d -> p (t d)").bitcast(I32),
+                in_=w_raw[c][:, values, :].rearrange("p t d -> p (t d)").bitcast(I32),
                 scalar=0x7FFF7FFF,
                 op=ALU.bitwise_and,
             )
-            for t in range(2 * u, 2 * u + 2):
-                for h in range(HALVES):
+            for t in range(first, first + width):
+                for d in range(0, D_IN, N_SUM):
                     nc.tensor.matmul(
                         out=column_sums[:],
                         lhsT=ones[:, 0:P],
-                        rhs=w_abs[:, c, t, h * N_MX : (h + 1) * N_MX],
-                        start=(c == 0 and t == 0 and h == 0),
-                        stop=(c == PASSES - 1 and t == PACK - 1 and h == HALVES - 1),
+                        rhs=w_abs[c][:, t, d : d + N_SUM],
+                        start=(c == 0 and t == 0 and d == 0),
+                        stop=(c == PASSES - 1 and t == PACK - 1 and d == D_IN - N_SUM),
                     )
 
         def regroup(copy, c, first, width):
@@ -162,11 +179,11 @@ def tile_ternarylinear_t_kernel(tc, x, weight, alpha, bias, grad_out, out):
                 out=w_grouped[:, c, first : first + width, :].rearrange(
                     "p (b i) t -> p b t i", i=4
                 ),
-                in_=w_raw[:, c, :, first : first + width].rearrange("p t (b i) -> p b t i", i=4),
+                in_=w_raw[c][:, :, first : first + width].rearrange("p t (b i) -> p b t i", i=4),
             )
 
         def magnitudes(c, first, width):
-            magnitude = work.tile([P, width * PACK], BF16, name="magnitude")
+            magnitude = work.tile([P, width * PACK], BF16, align_bytes=64, name="values")
             nc.vector.tensor_single_scalar(
                 out=magnitude[:].bitcast(I32),
                 in_=w_grouped[:, c, first : first + width, :]
@@ -177,14 +194,18 @@ def tile_ternarylinear_t_kernel(tc, x, weight, alpha, bias, grad_out, out):
             )
             return magnitude
 
-        add_chunk(0, 0)
-        add_chunk(0, 1)
-        regroup(nc.scalar.copy, 0, 0, N_MX)
-        add_chunk(1, 0)
-        add_chunk(1, 1)
-        regroup(nc.scalar.copy, 1, 0, N_MX)
+        add_chunk(0, 0, 2)
+        add_chunk(0, 2, 2)
+        regroup(nc.scalar.copy, 0, PIECE, PIECE)
+        regroup(nc.vector.tensor_copy, 0, 0, PIECE)
+        add_chunk(1, 0, 2)
+        add_chunk(1, 2, 1)
+        add_chunk(1, 3, 1)
+        regroup(nc.scalar.copy, 1, PIECE, PIECE)
+        regroup(nc.scalar.copy, 0, N_MX, PIECE)
         magnitude = magnitudes(0, 0, N_MX)
-        regroup(nc.vector.tensor_copy, 0, N_MX, PIECE)
+        regroup(nc.vector.tensor_copy, 1, 0, PIECE)
+        magnitude_1 = magnitudes(1, 0, N_MX)
 
         alpha_f32 = const.tile([P, 1], F32)
         nc.vector.tensor_copy(out=alpha_f32[:], in_=alpha_bf[:])
@@ -196,7 +217,7 @@ def tile_ternarylinear_t_kernel(tc, x, weight, alpha, bias, grad_out, out):
         nc.vector.tensor_scalar_mul(out=delta[:], in0=total[:], scalar1=0.7 / (D_OUT * D_IN))
 
         def masks(width, magnitude):
-            mask = work.tile([P, width * PACK], BF16, name="mask")
+            mask = magnitude
             nc.vector.tensor_scalar(
                 out=mask[:],
                 in0=magnitude[:],
@@ -208,7 +229,7 @@ def tile_ternarylinear_t_kernel(tc, x, weight, alpha, bias, grad_out, out):
             return mask
 
         def ternarise(c, first, width, mask):
-            ternary = work.tile([P, width * PACK], BF16, align_bytes=64, name="ternary")
+            ternary = mask
             nc.vector.scalar_tensor_tensor(
                 out=ternary[:].bitcast(I32),
                 in0=w_grouped[:, c, first : first + width, :]
@@ -232,13 +253,11 @@ def tile_ternarylinear_t_kernel(tc, x, weight, alpha, bias, grad_out, out):
             transpose_unit(unit)
 
         mask = masks(N_MX, magnitude)
-        magnitude = magnitudes(1, 0, N_MX)
+        mask_1 = masks(N_MX, magnitude_1)
         left = ternarise(0, 0, N_MX, mask)
         quantise_unit(0)
         quantise_weight(0, 0, N_MX, left)
-        mask = masks(N_MX, magnitude)
-        quantise_unit(1)
-        left = ternarise(1, 0, N_MX, mask)
+        left = ternarise(1, 0, N_MX, mask_1)
 
         pieces = [(c, first) for c in range(PASSES) for first in range(N_MX, D_IN, PIECE)]
         ready = {}
@@ -262,33 +281,46 @@ def tile_ternarylinear_t_kernel(tc, x, weight, alpha, bias, grad_out, out):
                 ready["mask"] = masks(PIECE, magnitudes(c, first, PIECE))
 
         accs = []
-        for tile in range(GROUP):
+        for tile in range(HALF):
             acc = sums.tile([P, N_MX], F32, name="acc")
             multiply(acc, tile, 0, 0)
             accs.append(acc)
-        for unit in range(AHEAD, LEAD):
+        for unit in BETWEEN[0]:
             transpose_unit(unit)
         quantise_weight(1, 0, N_MX, left)
+        quantise_unit(1)
+        for tile in range(HALF):
+            multiply(accs[tile], tile, 1, 0)
+        for unit in BETWEEN[1]:
+            transpose_unit(unit)
 
-        blocks = [(0, j) for j in range(EARLY)]
+        def half_block(j, h):
+            return [(GROUP * j + i, h) for i in range(GROUP)]
+
+        blocks = [half_block(j, 0) for j in range(EARLY)]
         for j in range(GROUPS):
-            blocks.append((1, j))
+            blocks.append(half_block(j, 1))
             if EARLY + j < GROUPS:
-                blocks.append((0, EARLY + j))
+                blocks.append(half_block(EARLY + j, 0))
+        first_use = {}
+        for b, block in enumerate(blocks):
+            for tile, h in block:
+                first_use.setdefault(tile // HALF, b)
         next_unit = LEAD
+        next_quantised = GROUP // HALF
         number = 0
-        for b, (h, j) in enumerate(blocks):
-            for i in range(GROUP):
-                tile = GROUP * j + i
-                if b == 0:
-                    acc = accs[i]
-                    multiply(acc, tile, 1, 0)
+        for b, block in enumerate(blocks):
+            for i, (tile, h) in enumerate(block):
+                if tile < HALF and h == 0:
+                    acc = accs[tile]
                 else:
                     acc = sums.tile([P, N_MX], F32, name="acc")
                     for c in range(PASSES):
                         multiply(acc, tile, c, h)
-                if i % 2 == 0 and b + 1 < len(blocks) and blocks[b + 1][0] == 0:
-                    quantise_unit(2 * blocks[b + 1][1] + i // 2)
+                if i % 2 == 0 and next_quantised < UNITS:
+                    if first_use[next_quantised] == b + 1:
+                        quantise_unit(next_quantised)
+                        next_quantised += 1
                 if i % 2 == 1 and b < EARLY:
                     weight_step(number)
                     number += 1

@@ -55,19 +55,16 @@ def tile_ternarylinear_t_kernel(tc, x, weight, alpha, bias, grad_out, out):
         out_view = out.flatten_outer_dims().rearrange("(p n) d -> p n d", n=TILES)
         w_view = weight.rearrange("(c u p e) d -> p c u (e d)", c=PASSES, u=2, p=P, e=2)
 
-        alpha_bf = const.tile([P, 1], BF16)
-        nc.scalar.dma_start(out=alpha_bf[:], in_=alpha.partition_broadcast(P))
+        alpha_row = const.tile([P, 2], BF16)
+        nc.vector.memset(alpha_row[:], 0.0)
+        nc.scalar.dma_start(out=alpha_row[0:1, 0:1], in_=alpha.rearrange("(a b) -> a b", a=1))
         w_raw = []
         for c in range(PASSES):
             w_tile = results.tile([P, PACK, D_IN], BF16, name="result")
             for u in range(2):
-                halves = 2 if c == PASSES - 1 and u == 1 else 1
-                width = 2 // halves
-                for e in range(0, 2, width):
-                    t = 2 * u + e
+                for e in range(2):
                     nc.sync.dma_start(
-                        out=w_tile[:, t : t + width, :].rearrange("p e d -> p (e d)"),
-                        in_=w_view[:, c, u, e * D_IN : (e + width) * D_IN],
+                        out=w_tile[:, 2 * u + e, :], in_=w_view[:, c, u, e * D_IN : (e + 1) * D_IN]
                     )
             w_raw.append(w_tile)
         g_raw = []
@@ -156,23 +153,21 @@ def tile_ternarylinear_t_kernel(tc, x, weight, alpha, bias, grad_out, out):
         w_grouped = keep.tile([P, PASSES, D_IN, PACK], BF16, align_bytes=64)
         column_sums = sums.tile([P, N_SUM], F32, name="acc")
 
-        def add_chunk(c, first, width):
-            values = slice(first, first + width)
+        def add_chunk(c, t):
             nc.vector.tensor_single_scalar(
-                out=w_abs[c][:, values, :].rearrange("p t d -> p (t d)").bitcast(I32),
-                in_=w_raw[c][:, values, :].rearrange("p t d -> p (t d)").bitcast(I32),
+                out=w_abs[c][:, t, :].bitcast(I32),
+                in_=w_raw[c][:, t, :].bitcast(I32),
                 scalar=0x7FFF7FFF,
                 op=ALU.bitwise_and,
             )
-            for t in range(first, first + width):
-                for d in range(0, D_IN, N_SUM):
-                    nc.tensor.matmul(
-                        out=column_sums[:],
-                        lhsT=ones[:, 0:P],
-                        rhs=w_abs[c][:, t, d : d + N_SUM],
-                        start=(c == 0 and t == 0 and d == 0),
-                        stop=(c == PASSES - 1 and t == PACK - 1 and d == D_IN - N_SUM),
-                    )
+            for d in range(0, D_IN, N_SUM):
+                nc.tensor.matmul(
+                    out=column_sums[:],
+                    lhsT=ones[:, 0:P],
+                    rhs=w_abs[c][:, t, d : d + N_SUM],
+                    start=(c == 0 and t == 0 and d == 0),
+                    stop=(c == PASSES - 1 and t == PACK - 1 and d == D_IN - N_SUM),
+                )
 
         def regroup(copy, c, first, width):
             copy(
@@ -194,21 +189,23 @@ def tile_ternarylinear_t_kernel(tc, x, weight, alpha, bias, grad_out, out):
             )
             return magnitude
 
-        add_chunk(0, 0, 2)
-        add_chunk(0, 2, 2)
+        for t in range(PACK):
+            add_chunk(0, t)
         regroup(nc.scalar.copy, 0, PIECE, PIECE)
-        regroup(nc.vector.tensor_copy, 0, 0, PIECE)
-        add_chunk(1, 0, 2)
-        add_chunk(1, 2, 1)
-        add_chunk(1, 3, 1)
-        regroup(nc.scalar.copy, 1, PIECE, PIECE)
         regroup(nc.scalar.copy, 0, N_MX, PIECE)
+        regroup(nc.vector.tensor_copy, 0, 0, PIECE)
+        alpha_bank = sums.tile([P, 2], F32, name="acc")
+        nc.tensor.matmul(
+            out=alpha_bank[:], lhsT=ones[:, 0:P], rhs=alpha_row[:], start=True, stop=True
+        )
+        alpha_f32 = const.tile([P, 1], F32)
+        nc.vector.tensor_copy(out=alpha_f32[:], in_=alpha_bank[:, 0:1])
+        for t in range(PACK):
+            add_chunk(1, t)
+        regroup(nc.scalar.copy, 1, PIECE, PIECE)
         magnitude = magnitudes(0, 0, N_MX)
         regroup(nc.vector.tensor_copy, 1, 0, PIECE)
-        magnitude_1 = magnitudes(1, 0, N_MX)
 
-        alpha_f32 = const.tile([P, 1], F32)
-        nc.vector.tensor_copy(out=alpha_f32[:], in_=alpha_bf[:])
         total = const.tile([P, 1], F32)
         nc.vector.tensor_reduce(
             out=total[:], in_=column_sums[:], axis=mybir.AxisListType.X, op=ALU.add
@@ -253,10 +250,11 @@ def tile_ternarylinear_t_kernel(tc, x, weight, alpha, bias, grad_out, out):
             transpose_unit(unit)
 
         mask = masks(N_MX, magnitude)
-        mask_1 = masks(N_MX, magnitude_1)
+        magnitude_1 = magnitudes(1, 0, N_MX)
         left = ternarise(0, 0, N_MX, mask)
         quantise_unit(0)
         quantise_weight(0, 0, N_MX, left)
+        mask_1 = masks(N_MX, magnitude_1)
         left = ternarise(1, 0, N_MX, mask_1)
 
         pieces = [(c, first) for c in range(PASSES) for first in range(N_MX, D_IN, PIECE)]

@@ -32,7 +32,8 @@ PIECE = 256
 BETWEEN = ((6,), (7,))
 EARLY = 6
 N_SUM = 256
-WARM = 4
+WARM = 4 * N_MX
+KEEP_WARM = N_MX + P
 
 FLOPS = 2 * TOKENS * D_OUT * D_IN
 BYTES = TOKENS * D_OUT * 2 + D_OUT * D_IN * 2 + 2 + TOKENS * D_IN * 4
@@ -56,7 +57,7 @@ def tile_ternarylinear_t_kernel(tc, x, weight, alpha, bias, grad_out, out):
         w_view = weight.rearrange("(c u p e) d -> p c u (e d)", c=PASSES, u=2, p=P, e=2)
 
         alpha_row = const.tile([P, 2], BF16)
-        nc.vector.memset(alpha_row[:], 0.0)
+        nc.gpsimd.memset(alpha_row[:], 0.0)
         nc.scalar.dma_start(out=alpha_row[0:1, 0:1], in_=alpha.rearrange("(a b) -> a b", a=1))
         w_raw = []
         for c in range(PASSES):
@@ -88,8 +89,19 @@ def tile_ternarylinear_t_kernel(tc, x, weight, alpha, bias, grad_out, out):
         make_identity(nc, identity[:])
 
         warm = sums.tile([P, N_MX], F32, name="acc")
-        for i in range(WARM):
-            nc.tensor.matmul(out=warm[:], lhsT=ones[:, 0:P], rhs=ones[:], start=True, stop=True)
+
+        def keep_warm(columns):
+            for first in range(0, columns, N_MX):
+                width = min(N_MX, columns - first)
+                nc.tensor.matmul(
+                    out=warm[:, 0:width],
+                    lhsT=ones[:, 0:P],
+                    rhs=ones[:, 0:width],
+                    start=True,
+                    stop=True,
+                )
+
+        keep_warm(WARM)
 
         g_codes = keep.tile([P, UNITS, HALF * PASSES * P], U32, align_bytes=64)
         g_scales = keep.tile([P, UNITS, HALF * PASSES * P], U8, align_bytes=64)
@@ -189,20 +201,21 @@ def tile_ternarylinear_t_kernel(tc, x, weight, alpha, bias, grad_out, out):
             )
             return magnitude
 
-        for t in range(PACK):
-            add_chunk(0, t)
-        regroup(nc.scalar.copy, 0, PIECE, PIECE)
-        regroup(nc.scalar.copy, 0, N_MX, PIECE)
-        regroup(nc.vector.tensor_copy, 0, 0, PIECE)
+        add_chunk(0, 0)
+        add_chunk(0, 1)
         alpha_bank = sums.tile([P, 2], F32, name="acc")
         nc.tensor.matmul(
             out=alpha_bank[:], lhsT=ones[:, 0:P], rhs=alpha_row[:], start=True, stop=True
         )
-        alpha_f32 = const.tile([P, 1], F32)
-        nc.vector.tensor_copy(out=alpha_f32[:], in_=alpha_bank[:, 0:1])
+        add_chunk(0, 2)
+        add_chunk(0, 3)
+        regroup(nc.scalar.copy, 0, PIECE, PIECE)
+        regroup(nc.scalar.copy, 0, 0, PIECE)
         for t in range(PACK):
             add_chunk(1, t)
         regroup(nc.scalar.copy, 1, PIECE, PIECE)
+        alpha_f32 = const.tile([P, 1], F32)
+        nc.vector.tensor_copy(out=alpha_f32[:], in_=alpha_bank[:, 0:1])
         magnitude = magnitudes(0, 0, N_MX)
         regroup(nc.vector.tensor_copy, 1, 0, PIECE)
 
@@ -248,6 +261,7 @@ def tile_ternarylinear_t_kernel(tc, x, weight, alpha, bias, grad_out, out):
 
         for unit in range(AHEAD):
             transpose_unit(unit)
+            keep_warm(KEEP_WARM)
 
         mask = masks(N_MX, magnitude)
         magnitude_1 = magnitudes(1, 0, N_MX)
@@ -261,11 +275,11 @@ def tile_ternarylinear_t_kernel(tc, x, weight, alpha, bias, grad_out, out):
         ready = {}
 
         def weight_step(number):
-            if number < len(pieces) - 1:
-                c, first = pieces[number + 1]
+            if number < len(pieces):
+                c, first = pieces[number]
                 regroup(nc.vector.tensor_copy, c, first, PIECE)
                 return
-            i, odd = divmod(number - (len(pieces) - 1), 2)
+            i, odd = divmod(number - len(pieces), 2)
             if odd:
                 if i < len(pieces):
                     c, first = pieces[i]
@@ -319,7 +333,7 @@ def tile_ternarylinear_t_kernel(tc, x, weight, alpha, bias, grad_out, out):
                     if first_use[next_quantised] == b + 1:
                         quantise_unit(next_quantised)
                         next_quantised += 1
-                if i % 2 == 1 and b < EARLY:
+                if b < EARLY and (i % 2 == 1 or (i == 2 and b == 1)):
                     weight_step(number)
                     number += 1
                 store(acc, tile, h, i % 2 == 0 or (b < EARLY and i == 1))

@@ -103,10 +103,10 @@ def tile_ternarylinear_t_kernel(tc, x, weight, alpha, bias, grad_out, out):
 
         keep_warm(WARM)
 
-        g_codes = keep.tile([P, UNITS, HALF * PASSES * P], U32, align_bytes=64)
-        g_scales = keep.tile([P, UNITS, HALF * PASSES * P], U8, align_bytes=64)
-        w_codes = keep.tile([P, PASSES, D_IN], U32, align_bytes=64)
-        w_scales = keep.tile([P, PASSES, D_IN], U8, align_bytes=64)
+        g_codes = keep.tile([P, UNITS, HALF * PASSES * P], U32, align_bytes=256)
+        g_scales = keep.tile([P, UNITS, HALF * PASSES * P], U8, align_bytes=256)
+        w_codes = keep.tile([P, PASSES, D_IN], U32, align_bytes=256)
+        w_scales = keep.tile([P, PASSES, D_IN], U8, align_bytes=256)
         g_grouped = {}
 
         def transpose_unit(unit):
@@ -285,12 +285,13 @@ def tile_ternarylinear_t_kernel(tc, x, weight, alpha, bias, grad_out, out):
                     c, first = pieces[i]
                     ready["ternary"] = ternarise(c, first, PIECE, ready["mask"])
                 return
-            if 0 < i <= len(pieces):
+            if i < len(pieces):
+                magnitude = magnitudes(pieces[i][0], pieces[i][1], PIECE)
+            if i > 0:
                 c, first = pieces[i - 1]
                 quantise_weight(c, first, PIECE, ready["ternary"])
             if i < len(pieces):
-                c, first = pieces[i]
-                ready["mask"] = masks(PIECE, magnitudes(c, first, PIECE))
+                ready["mask"] = masks(PIECE, magnitude)
 
         accs = []
         for tile in range(HALF):

@@ -63,9 +63,13 @@ def tile_ternarylinear_t_kernel(tc, x, weight, alpha, bias, grad_out, out):
         for c in range(PASSES):
             w_tile = results.tile([P, PACK, D_IN], BF16, name="result")
             for u in range(2):
-                for e in range(2):
+                values_a_load = 1 if c == PASSES - 1 and u == 1 else 2
+                for e in range(0, 2, values_a_load):
                     nc.sync.dma_start(
-                        out=w_tile[:, 2 * u + e, :], in_=w_view[:, c, u, e * D_IN : (e + 1) * D_IN]
+                        out=w_tile[:, 2 * u + e : 2 * u + e + values_a_load, :].rearrange(
+                            "p e d -> p (e d)"
+                        ),
+                        in_=w_view[:, c, u, e * D_IN : (e + values_a_load) * D_IN],
                     )
             w_raw.append(w_tile)
         g_raw = []
@@ -153,13 +157,17 @@ def tile_ternarylinear_t_kernel(tc, x, weight, alpha, bias, grad_out, out):
             )
 
         def store(acc, tile, h, on_scalar):
-            d_cols = slice(h * N_MX, (h + 1) * N_MX)
+            steps = 2 if tile == TILES - 1 and h == HALVES - 1 else 1
+            width = N_MX // steps
             result = half_rows.tile([P, N_MX], F32, name="half_row")
-            if on_scalar:
-                nc.scalar.copy(out=result[:], in_=acc[:])
-            else:
-                nc.vector.tensor_copy(out=result[:], in_=acc[:])
-            nc.sync.dma_start(out=out_view[:, tile, d_cols], in_=result[:])
+            for step in range(steps):
+                cols = slice(step * width, (step + 1) * width)
+                if on_scalar:
+                    nc.scalar.copy(out=result[:, cols], in_=acc[:, cols])
+                else:
+                    nc.vector.tensor_copy(out=result[:, cols], in_=acc[:, cols])
+                d_cols = slice(h * N_MX + cols.start, h * N_MX + cols.stop)
+                nc.sync.dma_start(out=out_view[:, tile, d_cols], in_=result[:, cols])
 
         w_abs = [results.tile([P, PACK, D_IN], BF16, name="result") for c in range(PASSES)]
         w_grouped = keep.tile([P, PASSES, D_IN, PACK], BF16, align_bytes=64)
@@ -271,27 +279,20 @@ def tile_ternarylinear_t_kernel(tc, x, weight, alpha, bias, grad_out, out):
         mask_1 = masks(N_MX, magnitude_1)
         left = ternarise(1, 0, N_MX, mask_1)
 
-        pieces = [(c, first) for c in range(PASSES) for first in range(N_MX, D_IN, PIECE)]
-        ready = {}
+        right = {}
 
         def weight_step(number):
-            if number < len(pieces):
-                c, first = pieces[number]
-                regroup(nc.vector.tensor_copy, c, first, PIECE)
-                return
-            i, odd = divmod(number - len(pieces), 2)
-            if odd:
-                if i < len(pieces):
-                    c, first = pieces[i]
-                    ready["ternary"] = ternarise(c, first, PIECE, ready["mask"])
-                return
-            if i < len(pieces):
-                magnitude = magnitudes(pieces[i][0], pieces[i][1], PIECE)
-            if i > 0:
-                c, first = pieces[i - 1]
-                quantise_weight(c, first, PIECE, ready["ternary"])
-            if i < len(pieces):
-                ready["mask"] = masks(PIECE, magnitude)
+            step, c = divmod(number, PASSES)
+            if step == 0:
+                regroup(nc.vector.tensor_copy, c, N_MX, N_MX)
+            elif step == 1:
+                right[c] = magnitudes(c, N_MX, N_MX)
+            elif step == 2:
+                right[c] = masks(N_MX, right[c])
+            elif step == 3:
+                right[c] = ternarise(c, N_MX, N_MX, right[c])
+            else:
+                quantise_weight(c, N_MX, N_MX, right[c])
 
         accs = []
         for tile in range(HALF):
@@ -334,10 +335,10 @@ def tile_ternarylinear_t_kernel(tc, x, weight, alpha, bias, grad_out, out):
                     if first_use[next_quantised] == b + 1:
                         quantise_unit(next_quantised)
                         next_quantised += 1
-                if b < EARLY and (i % 2 == 1 or (i == 2 and b == 1)):
+                if number < 5 * PASSES and i % 2 == 1:
                     weight_step(number)
                     number += 1
-                store(acc, tile, h, i % 2 == 0 or (b < EARLY and i == 1))
+                store(acc, tile, h, i % 2 == 0 or (number < 5 * PASSES and i == 1))
             if next_unit < UNITS:
                 transpose_unit(next_unit)
                 next_unit += 1

from contextlib import ExitStack

from concourse import mybir
from concourse.masks import make_identity

F32 = mybir.dt.float32
BF16 = mybir.dt.bfloat16
U32 = mybir.dt.uint32
U8 = mybir.dt.uint8
I32 = mybir.dt.int32
E4M3X4 = mybir.dt.float8_e4m3fn_x4
E5M2X4 = mybir.dt.float8_e5m2_x4
ALU = mybir.AluOpType

P = 128
TOKENS = 4096
D_OUT = 1024
D_IN = 1024
PACK = 4
K_PASS = P * PACK
PASSES = D_OUT // K_PASS
N_MX = 512
HALVES = D_IN // N_MX
TILES = TOKENS // P
GROUP = 4
GROUPS = TILES // GROUP
AHEAD = 6
HALF = 2
UNITS = TILES // HALF
LEAD = 8
PIECE = 256
BETWEEN = ((6,), (7,))
EARLY = 6
N_SUM = 256
WARM = 4 * N_MX
KEEP_WARM = N_MX + P

FLOPS = 2 * TOKENS * D_OUT * D_IN
BYTES = TOKENS * D_OUT * 2 + D_OUT * D_IN * 2 + 2 + TOKENS * D_IN * 4


def tile_ternarylinear_t_kernel(tc, x, weight, alpha, bias, grad_out, out):
    nc = tc.nc
    with ExitStack() as stack:
        stack.enter_context(tc.manual_schedule())
        const = stack.enter_context(tc.tile_pool(name="const", bufs=1))
        keep = stack.enter_context(tc.tile_pool(name="keep", bufs=1))
        work = stack.enter_context(tc.tile_pool(name="work", bufs=3))
        g_pool = stack.enter_context(tc.tile_pool(name="g_pool", bufs=GROUPS + 1))
        results = stack.enter_context(tc.tile_pool(name="results", bufs=4))
        half_rows = stack.enter_context(tc.tile_pool(name="half_rows", bufs=20))
        flipped = stack.enter_context(tc.psum_pool(name="flipped", bufs=3))
        sums = stack.enter_context(tc.psum_pool(name="sums", bufs=5))

        g_view = grad_out.flatten_outer_dims().rearrange("(p n) o -> p n o", n=TILES)
        out_view = out.flatten_outer_dims().rearrange("(p n) d -> p n d", n=TILES)
        w_view = weight.rearrange("(c u p e) d -> p c u (e d)", c=PASSES, u=2, p=P, e=2)

        alpha_row = const.tile([P, 2], BF16)
        nc.gpsimd.memset(alpha_row[:], 0.0)
        nc.scalar.dma_start(out=alpha_row[0:1, 0:1], in_=alpha.rearrange("(a b) -> a b", a=1))
        w_raw = []
        for c in range(PASSES):
            w_tile = results.tile([P, PACK, D_IN], BF16, name="result")
            for u in range(2):
                values_a_load = 1 if c == PASSES - 1 and u == 1 else 2
                for e in range(0, 2, values_a_load):
                    nc.sync.dma_start(
                        out=w_tile[:, 2 * u + e : 2 * u + e + values_a_load, :].rearrange(
                            "p e d -> p (e d)"
                        ),
                        in_=w_view[:, c, u, e * D_IN : (e + values_a_load) * D_IN],
                    )
            w_raw.append(w_tile)
        g_raw = []
        for j in range(GROUPS):
            g_tile = g_pool.tile([P, GROUP * D_OUT], BF16, align_bytes=64, name="g_tile")
            tiles_a_load = HALF if j < GROUPS // 2 else GROUP
            for n in range(0, GROUP, tiles_a_load):
                nc.sync.dma_start(
                    out=g_tile[:, n * D_OUT : (n + tiles_a_load) * D_OUT].rearrange(
                        "p (n o) -> p n o", n=tiles_a_load
                    ),
                    in_=g_view[:, GROUP * j + n : GROUP * j + n + tiles_a_load, :],
                )
            g_raw.append(g_tile)

        ones = const.tile([P, N_MX], BF16)
        nc.vector.memset(ones[:], 1.0)
        table = const.tile([P, 1], BF16)
        nc.scalar.copy(out=table[:], in_=ones[:, 0:1])
        identity = const.tile([P, P], F32)
        make_identity(nc, identity[:])

        warm = sums.tile([P, N_MX], F32, name="acc")

        def keep_warm(columns):
            for first in range(0, columns, N_MX):
                width = min(N_MX, columns - first)
                nc.tensor.matmul(
                    out=warm[:, 0:width],
                    lhsT=ones[:, 0:P],
                    rhs=ones[:, 0:width],
                    start=True,
                    stop=True,
                )

        keep_warm(WARM)

        g_codes = keep.tile([P, UNITS, HALF * PASSES * P], U32, align_bytes=256)
        g_scales = keep.tile([P, UNITS, HALF * PASSES * P], U8, align_bytes=256)
        w_codes = keep.tile([P, PASSES, D_IN], U32, align_bytes=256)
        w_scales = keep.tile([P, PASSES, D_IN], U8, align_bytes=256)
        g_grouped = {}

        def transpose_unit(unit):
            j, half = divmod(unit, GROUP // HALF)
            words = g_raw[j][:].bitcast(F32)
            if half == 0:
                g_grouped[j] = g_pool.tile(
                    [P, GROUP * D_OUT], BF16, align_bytes=64, name="g_tile"
                )
            grouped_words = g_grouped[j][:, half * HALF * D_OUT : (half + 1) * HALF * D_OUT].bitcast(F32).rearrange(
                "p (n c m u) -> p n c m u", n=HALF, c=PASSES, m=P, u=2
            )
            for n in range(HALF):
                bank = flipped.tile([P, PASSES * 2, P], F32, name="bank")
                for cu in range(PASSES * 2):
                    first = ((half * HALF + n) * PASSES * 2 + cu) * P
                    nc.tensor.transpose(bank[:, cu, :], words[:, first : first + P], identity[:])
                nc.scalar.copy(
                    out=grouped_words[:, n],
                    in_=bank[:].rearrange("p (c u) m -> p c m u", u=2),
                )

        def quantise_unit(unit):
            nc.vector.quantize_mx(
                out=g_codes[:, unit, :].bitcast(E5M2X4),
                scales=g_scales[:, unit, :],
                in_=g_grouped[unit // 2][
                    :, unit % 2 * HALF * D_OUT : (unit % 2 + 1) * HALF * D_OUT
                ],
            )

        def multiply(acc, tile, c, h):
            d_cols = slice(h * N_MX, (h + 1) * N_MX)
            first = (tile % HALF * PASSES + c) * P
            m_cols = slice(first, first + P)
            nc.tensor.matmul_mx(
                out=acc[:],
                lhsT=g_codes[:, tile // HALF, m_cols].bitcast(E5M2X4),
                lhsT_scale=g_scales[:, tile // HALF, m_cols],
                rhs=w_codes[:, c, d_cols].bitcast(E4M3X4),
                rhs_scale=w_scales[:, c, d_cols],
                start=(c == 0),
                stop=(c == PASSES - 1),
            )

        def store(acc, tile, h, on_scalar):
            steps = 2 if tile == TILES - 1 and h == HALVES - 1 else 1
            width = N_MX // steps
            result = half_rows.tile([P, N_MX], F32, name="half_row")
            for step in range(steps):
                cols = slice(step * width, (step + 1) * width)
                if on_scalar:
                    nc.scalar.copy(out=result[:, cols], in_=acc[:, cols])
                else:
                    nc.vector.tensor_copy(out=result[:, cols], in_=acc[:, cols])
                d_cols = slice(h * N_MX + cols.start, h * N_MX + cols.stop)
                nc.sync.dma_start(out=out_view[:, tile, d_cols], in_=result[:, cols])

        w_abs = [results.tile([P, PACK, D_IN], BF16, name="result") for c in range(PASSES)]
        w_grouped = keep.tile([P, PASSES, D_IN, PACK], BF16, align_bytes=64)
        column_sums = sums.tile([P, N_SUM], F32, name="acc")

        def add_chunk(c, t):
            nc.vector.tensor_single_scalar(
                out=w_abs[c][:, t, :].bitcast(I32),
                in_=w_raw[c][:, t, :].bitcast(I32),
                scalar=0x7FFF7FFF,
                op=ALU.bitwise_and,
            )
            for d in range(0, D_IN, N_SUM):
                nc.tensor.matmul(
                    out=column_sums[:],
                    lhsT=ones[:, 0:P],
                    rhs=w_abs[c][:, t, d : d + N_SUM],
                    start=(c == 0 and t == 0 and d == 0),
                    stop=(c == PASSES - 1 and t == PACK - 1 and d == D_IN - N_SUM),
                )

        def regroup(copy, c, first, width):
            copy(
                out=w_grouped[:, c, first : first + width, :].rearrange(
                    "p (b i) t -> p b t i", i=4
                ),
                in_=w_raw[c][:, :, first : first + width].rearrange("p t (b i) -> p b t i", i=4),
            )

        def magnitudes(c, first, width):
            magnitude = work.tile([P, width * PACK], BF16, align_bytes=64, name="values")
            nc.vector.tensor_single_scalar(
                out=magnitude[:].bitcast(I32),
                in_=w_grouped[:, c, first : first + width, :]
                .rearrange("p d t -> p (d t)")
                .bitcast(I32),
                scalar=0x7FFF7FFF,
                op=ALU.bitwise_and,
            )
            return magnitude

        add_chunk(0, 0)
        add_chunk(0, 1)
        alpha_bank = sums.tile([P, 2], F32, name="acc")
        nc.tensor.matmul(
            out=alpha_bank[:], lhsT=ones[:, 0:P], rhs=alpha_row[:], start=True, stop=True
        )
        add_chunk(0, 2)
        add_chunk(0, 3)
        regroup(nc.scalar.copy, 0, PIECE, PIECE)
        regroup(nc.scalar.copy, 0, 0, PIECE)
        for t in range(PACK):
            add_chunk(1, t)
        regroup(nc.scalar.copy, 1, PIECE, PIECE)
        alpha_f32 = const.tile([P, 1], F32)
        nc.vector.tensor_copy(out=alpha_f32[:], in_=alpha_bank[:, 0:1])
        magnitude = magnitudes(0, 0, N_MX)
        regroup(nc.vector.tensor_copy, 1, 0, PIECE)

        total = const.tile([P, 1], F32)
        nc.vector.tensor_reduce(
            out=total[:], in_=column_sums[:], axis=mybir.AxisListType.X, op=ALU.add
        )
        delta = const.tile([P, 1], F32)
        nc.vector.tensor_scalar_mul(out=delta[:], in0=total[:], scalar1=0.7 / (D_OUT * D_IN))

        def masks(width, magnitude):
            mask = magnitude
            nc.vector.tensor_scalar(
                out=mask[:],
                in0=magnitude[:],
                scalar1=delta[:, 0:1],
                scalar2=alpha_f32[:, 0:1],
                op0=ALU.is_gt,
                op1=ALU.mult,
            )
            return mask

        def ternarise(c, first, width, mask):
            ternary = mask
            nc.vector.scalar_tensor_tensor(
                out=ternary[:].bitcast(I32),
                in0=w_grouped[:, c, first : first + width, :]
                .rearrange("p d t -> p (d t)")
                .bitcast(I32),
                scalar=-0x7FFF8000,
                in1=mask[:].bitcast(I32),
                op0=ALU.bitwise_and,
                op1=ALU.bitwise_xor,
            )
            return ternary

        def quantise_weight(c, first, width, ternary):
            nc.vector.quantize_mx(
                out=w_codes[:, c, first : first + width].bitcast(E4M3X4),
                scales=w_scales[:, c, first : first + width],
                in_=ternary[:],
            )

        for unit in range(AHEAD):
            transpose_unit(unit)
            keep_warm(KEEP_WARM)

        mask = masks(N_MX, magnitude)
        magnitude_1 = magnitudes(1, 0, N_MX)
        left = ternarise(0, 0, N_MX, mask)
        quantise_unit(0)
        quantise_weight(0, 0, N_MX, left)
        mask_1 = masks(N_MX, magnitude_1)
        left = ternarise(1, 0, N_MX, mask_1)

        right = {}

        def weight_step(number):
            step, c = divmod(number, PASSES)
            if step == 0:
                regroup(nc.vector.tensor_copy, c, N_MX, N_MX)
            elif step == 1:
                right[c] = magnitudes(c, N_MX, N_MX)
            elif step == 2:
                right[c] = masks(N_MX, right[c])
            elif step == 3:
                right[c] = ternarise(c, N_MX, N_MX, right[c])
            else:
                quantise_weight(c, N_MX, N_MX, right[c])

        accs = []
        for tile in range(HALF):
            acc = sums.tile([P, N_MX], F32, name="acc")
            multiply(acc, tile, 0, 0)
            accs.append(acc)
        for unit in BETWEEN[0]:
            transpose_unit(unit)
        quantise_weight(1, 0, N_MX, left)
        quantise_unit(1)
        for tile in range(HALF):
            multiply(accs[tile], tile, 1, 0)
        for unit in BETWEEN[1]:
            transpose_unit(unit)

        def half_block(j, h):
            return [(GROUP * j + i, h) for i in range(GROUP)]

        blocks = [half_block(j, 0) for j in range(EARLY)]
        for j in range(GROUPS):
            blocks.append(half_block(j, 1))
            if EARLY + j < GROUPS:
                blocks.append(half_block(EARLY + j, 0))
        first_use = {}
        for b, block in enumerate(blocks):
            for tile, h in block:
                first_use.setdefault(tile // HALF, b)
        next_unit = LEAD
        next_quantised = GROUP // HALF
        number = 0
        for b, block in enumerate(blocks):
            for i, (tile, h) in enumerate(block):
                if tile < HALF and h == 0:
                    acc = accs[tile]
                else:
                    acc = sums.tile([P, N_MX], F32, name="acc")
                    for c in range(PASSES):
                        multiply(acc, tile, c, h)
                if i % 2 == 0 and next_quantised < UNITS:
                    if first_use[next_quantised] == b + 1:
                        quantise_unit(next_quantised)
                        next_quantised += 1
                if number < 5 * PASSES and i % 2 == 1:
                    weight_step(number)
                    number += 1
                store(acc, tile, h, i % 2 == 0 or (number < 5 * PASSES and i == 1))
            if next_unit < UNITS:
                transpose_unit(next_unit)
                next_unit += 1
